import numpy as np
import ml_dtypes


def mxq(x, axis, fmt="e4m3"):
    dtype, down = {"e4m3": (ml_dtypes.float8_e4m3fn, 7), "e5m2": (ml_dtypes.float8_e5m2, 14)}[fmt]
    v = np.moveaxis(np.asarray(x, np.float32).astype(ml_dtypes.bfloat16).astype(np.float64), axis, -1)
    blocks = v.reshape(v.shape[:-1] + (-1, 32))
    amax = np.abs(blocks).max(-1, keepdims=True)
    byte = np.maximum(np.where(amax > 0, np.frexp(amax)[1] - 1 + 127, 0) - down, 1)
    scale = np.exp2(byte - 127.0)
    codes = (blocks / scale).astype(np.float32).astype(dtype).astype(np.float64)
    return np.moveaxis((codes * scale).reshape(v.shape), -1, axis)


WIDE = False


def mx_kscale(k):
    if not WIDE:
        return np.ones(k)
    levels = np.array([10, -10, 5, -5, 0])
    a = np.random.permutation(np.resize(levels, k // 512 * 4)).reshape(k // 512, 4)
    idx = np.arange(k)
    return np.exp2(a[idx // 512, idx % 128 // 32])


BF16 = ml_dtypes.bfloat16


def bf(x):
    return np.asarray(x, np.float32).astype(BF16)


def f64(x):
    return np.asarray(x).astype(np.float64)


B, T, C, H, D, R = 1, 1024, 2048, 16, 128, 512
EPS = 1e-6
THETA = 10000.0


def rmsnorm(v, w):
    var = np.mean(v * v, axis=-1, keepdims=True)
    return v * (1.0 / np.sqrt(var + EPS)) * w


def rope(v, cos, sin):
    re, im = v[..., 0::2], v[..., 1::2]
    c, s = cos[None, :, None, :], sin[None, :, None, :]
    return np.stack([re * c - im * s, re * s + im * c], axis=-1).reshape(v.shape)


def setup_inputs():
    s, t = mx_kscale(C), mx_kscale(R)
    ang = np.outer(np.arange(T), 1.0 / THETA ** (np.arange(0, D, 2) / D))
    return {"x": bf(np.random.standard_normal((B, T, C)) * s),
            "w_kv_down": bf(np.random.standard_normal((R, C)) / np.sqrt(C) / s[None, :] * t[:, None]),
            "w_kv_up": bf(np.random.standard_normal((2 * H * D, R)) / np.sqrt(R) / t[None, :]),
            "k_norm_w": bf(1.0 + 0.1 * np.random.standard_normal(D)),
            "freqs_cos": bf(np.cos(ang)), "freqs_sin": bf(np.sin(ang))}


def reference(x, w_kv_down, w_kv_up, k_norm_w, freqs_cos, freqs_sin):
    latent = mxq(f64(x), 2, "e4m3") @ mxq(f64(w_kv_down), 1, "e4m3").T
    kv = (mxq(latent, 2, "e4m3") @ mxq(f64(w_kv_up), 1, "e4m3").T).reshape(B, T, 2, H, D)
    xk, xv = kv[:, :, 0], kv[:, :, 1]
    return rope(rmsnorm(xk, f64(k_norm_w)), f64(freqs_cos), f64(freqs_sin)), xv

@@ -1,0 +1,258 @@
+from contextlib import ExitStack
+
+import concourse.mybir as mybir
+from concourse.masks import make_identity
+
+F32 = mybir.dt.float32
+BF16 = mybir.dt.bfloat16
+U32 = mybir.dt.uint32
+U8 = mybir.dt.uint8
+FP8X4 = mybir.dt.float8_e4m3fn_x4
+ALU = mybir.AluOpType
+ACT = mybir.ActivationFunctionType
+
+P = 128
+PACK = 4
+K_PASS = P * PACK
+BANK = 512
+
+TOKENS, C, R, HEADS, D = 1024, 2048, 512, 16, 128
+EPS = 1e-6
+TOKEN_TILES = TOKENS // P
+C_PASSES = C // K_PASS
+R_GROUPS = R // P
+HEADS_PER_BANK = BANK // D
+BANKS_PER_HALF = HEADS * D // BANK
+WU_CHUNKS = 4
+BLOCKS_PER_CHUNK = 2 * HEADS * D // P // WU_CHUNKS
+
+FLOPS = 2 * TOKENS * C * R + 2 * TOKENS * R * 2 * HEADS * D
+
+
+def transpose_and_quantise(nc, psum, grouped, ident, blocks, codes, scales):
+    grouped_words = grouped.bitcast(F32).rearrange("p (a r u) -> p a r u", r=P, u=2)
+    for pair in range(len(blocks) // 2):
+        bank = psum.tile([P, 2, 2, P], F32, tag="bank")
+        for a in range(2):
+            words = blocks[2 * pair + a].bitcast(F32)
+            for u in range(2):
+                nc.tensor.transpose(bank[:, a, u, :], words[:, u * P : (u + 1) * P], ident)
+        copy_out = nc.vector.tensor_copy if pair % 4 == 3 else nc.scalar.copy
+        copy_out(
+            out=grouped_words[:, 2 * pair : 2 * pair + 2, :, :],
+            in_=bank[:].rearrange("p a u r -> p a r u"),
+        )
+    nc.vector.quantize_mx(out=codes.bitcast(FP8X4), scales=scales, in_=grouped)
+
+
+def tile_mla_pa_kernel(
+    tc, x, w_kv_down, w_kv_up, k_norm_w, freqs_cos, freqs_sin, out_0, out_1
+):
+    nc = tc.nc
+    x_view = x.flatten_outer_dims().rearrange("(p i) c -> p i c", i=TOKEN_TILES)
+    k_out_view = out_0.flatten_outer_dims().rearrange(
+        "(p i h) d -> p i (h d)", i=TOKEN_TILES, h=HEADS
+    )
+    v_out_view = out_1.flatten_outer_dims().rearrange(
+        "(p i h) d -> p i (h d)", i=TOKEN_TILES, h=HEADS
+    )
+
+    with ExitStack() as pools:
+        keep = pools.enter_context(tc.tile_pool(name="keep", bufs=1))
+        weight_stage = pools.enter_context(tc.tile_pool(name="weight_stage", bufs=2))
+        token_stage = pools.enter_context(tc.tile_pool(name="token_stage", bufs=2))
+        stats = pools.enter_context(tc.tile_pool(name="stats", bufs=4))
+        results = pools.enter_context(tc.tile_pool(name="results", bufs=2))
+        psum = pools.enter_context(tc.psum_pool(name="psum", bufs=8))
+
+        wd_rows = w_kv_down.rearrange("(u q e) c -> e q u c", u=2, e=2)
+        wd_raw = []
+        for e in range(2):
+            wd_half = keep.tile([P, 2, C], BF16, name="wd_raw%d" % e)
+            nc.sync.dma_start(out=wd_half[:], in_=wd_rows[e])
+            wd_raw.append(wd_half)
+        x_raw = []
+        for pair in range(TOKEN_TILES // 2):
+            x_raw.append(keep.tile([P, 2, C], BF16, name="x_raw%d" % pair))
+        nc.sync.dma_start(out=x_raw[0][:], in_=x_view[:, 0:2, :])
+        wu_blocks = w_kv_up.rearrange("(n p) r -> p n r", p=P)
+        wu_raw = []
+        for chunk in range(WU_CHUNKS):
+            wu_part = keep.tile([P, BLOCKS_PER_CHUNK, R], BF16, name="wu_raw%d" % chunk)
+            nc.sync.dma_start(
+                out=wu_part[:],
+                in_=wu_blocks[:, chunk * BLOCKS_PER_CHUNK : (chunk + 1) * BLOCKS_PER_CHUNK, :],
+            )
+            wu_raw.append(wu_part)
+        for pair in range(1, TOKEN_TILES // 2):
+            nc.sync.dma_start(out=x_raw[pair][:], in_=x_view[:, 2 * pair : 2 * pair + 2, :])
+
+        cos_bf = keep.tile([P, TOKEN_TILES, D // 2], BF16, name="cos_bf")
+        sin_bf = keep.tile([P, TOKEN_TILES, D // 2], BF16, name="sin_bf")
+        gain_bf = keep.tile([P, D], BF16, name="gain_bf")
+        nc.scalar.dma_start(out=cos_bf[:], in_=freqs_cos.rearrange("(p i) j -> p i j", i=TOKEN_TILES))
+        nc.scalar.dma_start(out=sin_bf[:], in_=freqs_sin.rearrange("(p i) j -> p i j", i=TOKEN_TILES))
+        nc.scalar.dma_start(out=gain_bf[:], in_=k_norm_w.partition_broadcast(P))
+
+        ident = keep.tile([P, P], F32, name="ident")
+        make_identity(nc, ident[:])
+        one = keep.tile([P, 1], F32, name="one")
+        nc.vector.memset(one[:], 1.0)
+        nc.scalar.activation(out=one[:], in_=one[:], func=ACT.Sqrt)
+
+        own = keep.tile([P, TOKEN_TILES, D // 2, 2], F32, name="own")
+        partner = keep.tile([P, TOKEN_TILES, 2, D // 2], F32, name="partner")
+        neg_gain = keep.tile([P, D], BF16, name="neg_gain")
+        table_shape = [P, TOKEN_TILES, D // 2]
+        nc.gpsimd.tensor_scalar(
+            out=neg_gain[:], in0=gain_bf[:], scalar1=-1.0, scalar2=0.0, op0=ALU.mult, op1=ALU.add
+        )
+        nc.gpsimd.tensor_tensor(
+            out=own[:],
+            in0=cos_bf[:].unsqueeze(3).to_broadcast(table_shape + [2]),
+            in1=gain_bf[:].rearrange("p (j e) -> p j e", e=2).unsqueeze(1).to_broadcast(table_shape + [2]),
+            op=ALU.mult,
+        )
+        nc.gpsimd.tensor_tensor(
+            out=partner[:, :, 0, :],
+            in0=sin_bf[:],
+            in1=neg_gain[:].rearrange("p (j e) -> p e j", e=2)[:, 1, :].unsqueeze(1).to_broadcast(table_shape),
+            op=ALU.mult,
+        )
+        nc.gpsimd.tensor_tensor(
+            out=partner[:, :, 1, :],
+            in0=sin_bf[:],
+            in1=gain_bf[:].rearrange("p (j e) -> p e j", e=2)[:, 0, :].unsqueeze(1).to_broadcast(table_shape),
+            op=ALU.mult,
+        )
+
+        wd_codes = keep.tile([P, C_PASSES, R_GROUPS, P], U32, name="wd_codes", align_bytes=64)
+        wd_scales = keep.tile([P, C_PASSES, R_GROUPS, P], U8, name="wd_scales", align_bytes=64)
+        for first in range(0, C_PASSES, 2):
+            blocks = [
+                wd_raw[t % 2][:, t // 2, g * K_PASS : (g + 1) * K_PASS]
+                for g in range(first, first + 2)
+                for t in range(R_GROUPS)
+            ]
+            grouped = weight_stage.tile([P, len(blocks) * K_PASS], BF16, tag="grouped", align_bytes=64)
+            transpose_and_quantise(
+                nc, psum, grouped[:], ident[:], blocks,
+                wd_codes[:, first : first + 2, :, :].rearrange("p g t q -> p (g t q)"),
+                wd_scales[:, first : first + 2, :, :].rearrange("p g t q -> p (g t q)"),
+            )
+
+        def latent_of_tile(i):
+            x_codes = token_stage.tile([P, C_PASSES, P], U32, tag="x_codes", align_bytes=64)
+            x_scales = token_stage.tile([P, C_PASSES, P], U8, tag="x_scales", align_bytes=64)
+            x_grouped = token_stage.tile([P, C_PASSES * K_PASS], BF16, tag="x_grouped", align_bytes=64)
+            blocks = [x_raw[i // 2][:, i % 2, g * K_PASS : (g + 1) * K_PASS] for g in range(C_PASSES)]
+            transpose_and_quantise(
+                nc, psum, x_grouped[:], ident[:], blocks,
+                x_codes[:].rearrange("p g r -> p (g r)"),
+                x_scales[:].rearrange("p g r -> p (g r)"),
+            )
+            lat_bank = psum.tile([P, R_GROUPS, P], F32, tag="bank")
+            for t in range(R_GROUPS):
+                for g in range(C_PASSES):
+                    nc.tensor.matmul_mx(
+                        out=lat_bank[:, t, :],
+                        lhsT=wd_codes[:, g, t, :].bitcast(FP8X4),
+                        lhsT_scale=wd_scales[:, g, t, :],
+                        rhs=x_codes[:, g, :].bitcast(FP8X4),
+                        rhs_scale=x_scales[:, g, :],
+                        start=(g == 0),
+                        stop=(g == C_PASSES - 1),
+                    )
+            lat_grouped = token_stage.tile([P, P, R_GROUPS], BF16, tag="lat_grouped", align_bytes=64)
+            nc.vector.tensor_copy(out=lat_grouped[:], in_=lat_bank[:].rearrange("p t r -> p r t"))
+            lat_codes = token_stage.tile([P, P], U32, tag="lat_codes", align_bytes=64)
+            lat_scales = token_stage.tile([P, P], U8, tag="lat_scales", align_bytes=64)
+            nc.vector.quantize_mx(
+                out=lat_codes[:].bitcast(FP8X4),
+                scales=lat_scales[:],
+                in_=lat_grouped[:].rearrange("p r t -> p (r t)"),
+            )
+            return lat_codes, lat_scales
+
+        latent = latent_of_tile(0)
+
+        wu_codes = keep.tile([P, 2 * HEADS * D], U32, name="wu_codes", align_bytes=64)
+        wu_scales = keep.tile([P, 2 * HEADS * D], U8, name="wu_scales", align_bytes=64)
+        for chunk in range(WU_CHUNKS):
+            blocks = [wu_raw[chunk][:, n, :] for n in range(BLOCKS_PER_CHUNK)]
+            columns = slice(chunk * BLOCKS_PER_CHUNK * P, (chunk + 1) * BLOCKS_PER_CHUNK * P)
+            grouped = weight_stage.tile([P, len(blocks) * K_PASS], BF16, tag="grouped", align_bytes=64)
+            transpose_and_quantise(
+                nc, psum, grouped[:], ident[:], blocks, wu_codes[:, columns], wu_scales[:, columns]
+            )
+
+        def project(bank, lat, first_feature):
+            lat_codes, lat_scales = lat
+            nc.tensor.matmul_mx(
+                out=bank,
+                lhsT=lat_codes[:].bitcast(FP8X4),
+                lhsT_scale=lat_scales[:],
+                rhs=wu_codes[:, first_feature : first_feature + BANK].bitcast(FP8X4),
+                rhs_scale=wu_scales[:, first_feature : first_feature + BANK],
+                start=True,
+                stop=True,
+            )
+
+        for i in range(TOKEN_TILES):
+            next_latent = latent_of_tile(i + 1) if i + 1 < TOKEN_TILES else None
+
+            k_rot = results.tile([P, HEADS, D], F32, tag="k_rot", bufs=3)
+            crossed = results.tile([P, 2, HEADS, D // 2], F32, tag="crossed")
+            v_sb = results.tile([P, HEADS * D], F32, tag="v_sb", bufs=3)
+            for b in range(BANKS_PER_HALF):
+                heads = slice(b * HEADS_PER_BANK, (b + 1) * HEADS_PER_BANK)
+
+                k_bank = psum.tile([P, HEADS_PER_BANK, D // 2, 2], F32, tag="bank")
+                project(k_bank[:].rearrange("p h j e -> p (h j e)"), latent, b * BANK)
+                squares = stats.tile([P, HEADS_PER_BANK, D], BF16, tag="squares", bufs=2)
+                sumsq = stats.tile([P, HEADS_PER_BANK], F32, tag="sumsq")
+                rms = stats.tile([P, HEADS_PER_BANK], F32, tag="rms")
+                rstd = stats.tile([P, HEADS_PER_BANK], F32, tag="rstd")
+                for h in range(HEADS_PER_BANK):
+                    nc.scalar.activation(
+                        out=squares[:, h, :],
+                        in_=k_bank[:, h, :, :].rearrange("p j e -> p (j e)"),
+                        func=ACT.Square,
+                        accum_out=sumsq[:, h : h + 1],
+                    )
+                nc.scalar.activation(out=rms[:], in_=sumsq[:], func=ACT.Sqrt, scale=1.0 / D, bias=EPS)
+                nc.vector.reciprocal(out=rstd[:], in_=rms[:])
+                for h in range(HEADS_PER_BANK):
+                    head = b * HEADS_PER_BANK + h
+                    nc.vector.scalar_tensor_tensor(
+                        out=k_rot[:, head, :],
+                        in0=k_bank[:, h, :, :].rearrange("p j e -> p (j e)"),
+                        scalar=rstd[:, h : h + 1],
+                        in1=own[:, i, :, :].rearrange("p j e -> p (j e)"),
+                        op0=ALU.mult,
+                        op1=ALU.mult,
+                    )
+                    for e in range(2):
+                        nc.vector.scalar_tensor_tensor(
+                            out=crossed[:, e, head, :],
+                            in0=k_bank[:, h, :, 1 - e],
+                            scalar=rstd[:, h : h + 1],
+                            in1=partner[:, i, e, :],
+                            op0=ALU.mult,
+                            op1=ALU.mult,
+                        )
+                k_pairs = k_rot[:, heads, :].rearrange("p h (j e) -> p h j e", e=2)
+                nc.gpsimd.tensor_tensor(
+                    out=k_pairs,
+                    in0=k_pairs,
+                    in1=crossed[:, :, heads, :].rearrange("p e h j -> p h j e"),
+                    op=ALU.add,
+                )
+
+                v_bank = psum.tile([P, BANK], F32, tag="bank")
+                project(v_bank[:], latent, HEADS * D + b * BANK)
+                nc.scalar.copy(out=v_sb[:, b * BANK : (b + 1) * BANK], in_=v_bank[:])
+
+            nc.sync.dma_start(out=v_out_view[:, i, :], in_=v_sb[:])
+            nc.sync.dma_start(out=k_out_view[:, i, :], in_=k_rot[:].rearrange("p h d -> p (h d)"))
+            latent = next_latent

@@ -18,31 +18,30 @@ BANK = 512
 
 TOKENS, C, R, HEADS, D = 1024, 2048, 512, 16, 128
 EPS = 1e-6
+HALF = D // 2
 TOKEN_TILES = TOKENS // P
 C_PASSES = C // K_PASS
 R_GROUPS = R // P
 HEADS_PER_BANK = BANK // D
-BANKS_PER_HALF = HEADS * D // BANK
 WU_CHUNKS = 4
 BLOCKS_PER_CHUNK = 2 * HEADS * D // P // WU_CHUNKS
 
 FLOPS = 2 * TOKENS * C * R + 2 * TOKENS * R * 2 * HEADS * D
 
 
-def transpose_and_quantise(nc, psum, grouped, ident, blocks, codes, scales):
+def transpose_blocks(nc, psum, grouped, matrix, blocks):
     grouped_words = grouped.bitcast(F32).rearrange("p (a r u) -> p a r u", r=P, u=2)
     for pair in range(len(blocks) // 2):
         bank = psum.tile([P, 2, 2, P], F32, tag="bank")
         for a in range(2):
             words = blocks[2 * pair + a].bitcast(F32)
             for u in range(2):
-                nc.tensor.transpose(bank[:, a, u, :], words[:, u * P : (u + 1) * P], ident)
+                nc.tensor.transpose(bank[:, a, u, :], words[:, u * P : (u + 1) * P], matrix)
         copy_out = nc.vector.tensor_copy if pair % 4 == 3 else nc.scalar.copy
         copy_out(
             out=grouped_words[:, 2 * pair : 2 * pair + 2, :, :],
             in_=bank[:].rearrange("p a u r -> p a r u"),
         )
-    nc.vector.quantize_mx(out=codes.bitcast(FP8X4), scales=scales, in_=grouped)
 
 
 def tile_mla_pa_kernel(
@@ -57,13 +56,14 @@ def tile_mla_pa_kernel(
         "(p i h) d -> p i (h d)", i=TOKEN_TILES, h=HEADS
     )
 
-    with ExitStack() as pools:
-        keep = pools.enter_context(tc.tile_pool(name="keep", bufs=1))
-        weight_stage = pools.enter_context(tc.tile_pool(name="weight_stage", bufs=2))
-        token_stage = pools.enter_context(tc.tile_pool(name="token_stage", bufs=2))
-        stats = pools.enter_context(tc.tile_pool(name="stats", bufs=4))
-        results = pools.enter_context(tc.tile_pool(name="results", bufs=2))
-        psum = pools.enter_context(tc.psum_pool(name="psum", bufs=8))
+    with ExitStack() as stack:
+        stack.enter_context(tc.manual_schedule())
+        keep = stack.enter_context(tc.tile_pool(name="keep", bufs=1))
+        weight_stage = stack.enter_context(tc.tile_pool(name="weight_stage", bufs=3))
+        token_stage = stack.enter_context(tc.tile_pool(name="token_stage", bufs=2))
+        stats = stack.enter_context(tc.tile_pool(name="stats", bufs=4))
+        results = stack.enter_context(tc.tile_pool(name="results", bufs=3))
+        psum = stack.enter_context(tc.psum_pool(name="psum", bufs=8))
 
         wd_rows = w_kv_down.rearrange("(u q e) c -> e q u c", u=2, e=2)
         wd_raw = []
@@ -87,70 +87,94 @@ def tile_mla_pa_kernel(
         for pair in range(1, TOKEN_TILES // 2):
             nc.sync.dma_start(out=x_raw[pair][:], in_=x_view[:, 2 * pair : 2 * pair + 2, :])
 
-        cos_bf = keep.tile([P, TOKEN_TILES, D // 2], BF16, name="cos_bf")
-        sin_bf = keep.tile([P, TOKEN_TILES, D // 2], BF16, name="sin_bf")
-        gain_bf = keep.tile([P, D], BF16, name="gain_bf")
+        cos_bf = keep.tile([P, TOKEN_TILES, HALF], BF16, name="cos_bf")
+        sin_bf = keep.tile([P, TOKEN_TILES, HALF], BF16, name="sin_bf")
+        gain_bf = keep.tile([P, HALF, 2], BF16, name="gain_bf")
         nc.scalar.dma_start(out=cos_bf[:], in_=freqs_cos.rearrange("(p i) j -> p i j", i=TOKEN_TILES))
         nc.scalar.dma_start(out=sin_bf[:], in_=freqs_sin.rearrange("(p i) j -> p i j", i=TOKEN_TILES))
-        nc.scalar.dma_start(out=gain_bf[:], in_=k_norm_w.partition_broadcast(P))
+        nc.scalar.dma_start(
+            out=gain_bf[:].rearrange("p j e -> p (j e)"), in_=k_norm_w.partition_broadcast(P)
+        )
 
-        ident = keep.tile([P, P], F32, name="ident")
-        make_identity(nc, ident[:])
         one = keep.tile([P, 1], F32, name="one")
         nc.vector.memset(one[:], 1.0)
         nc.scalar.activation(out=one[:], in_=one[:], func=ACT.Sqrt)
+        ident = keep.tile([P, P], F32, name="ident")
+        make_identity(nc, ident[:])
+        split_pairs = keep.tile([P, 2, HALF], F32, name="split_pairs")
+        nc.vector.tensor_copy(out=split_pairs[:], in_=ident[:].rearrange("p (j e) -> p e j", e=2))
 
-        own = keep.tile([P, TOKEN_TILES, D // 2, 2], F32, name="own")
-        partner = keep.tile([P, TOKEN_TILES, 2, D // 2], F32, name="partner")
-        neg_gain = keep.tile([P, D], BF16, name="neg_gain")
-        table_shape = [P, TOKEN_TILES, D // 2]
+        rope_table = keep.tile([P, TOKEN_TILES, 4, HALF], F32, name="rope_table")
+        neg_gain = keep.tile([P, HALF, 2], BF16, name="neg_gain")
         nc.gpsimd.tensor_scalar(
             out=neg_gain[:], in0=gain_bf[:], scalar1=-1.0, scalar2=0.0, op0=ALU.mult, op1=ALU.add
         )
-        nc.gpsimd.tensor_tensor(
-            out=own[:],
-            in0=cos_bf[:].unsqueeze(3).to_broadcast(table_shape + [2]),
-            in1=gain_bf[:].rearrange("p (j e) -> p j e", e=2).unsqueeze(1).to_broadcast(table_shape + [2]),
-            op=ALU.mult,
-        )
-        nc.gpsimd.tensor_tensor(
-            out=partner[:, :, 0, :],
-            in0=sin_bf[:],
-            in1=neg_gain[:].rearrange("p (j e) -> p e j", e=2)[:, 1, :].unsqueeze(1).to_broadcast(table_shape),
-            op=ALU.mult,
-        )
-        nc.gpsimd.tensor_tensor(
-            out=partner[:, :, 1, :],
-            in0=sin_bf[:],
-            in1=gain_bf[:].rearrange("p (j e) -> p e j", e=2)[:, 0, :].unsqueeze(1).to_broadcast(table_shape),
-            op=ALU.mult,
-        )
+        plane_factors = [
+            (cos_bf, gain_bf[:, :, 0]),
+            (sin_bf, neg_gain[:, :, 1]),
+            (sin_bf, gain_bf[:, :, 0]),
+            (cos_bf, gain_bf[:, :, 1]),
+        ]
+        for plane, (angle, gain) in enumerate(plane_factors):
+            nc.gpsimd.tensor_tensor(
+                out=rope_table[:, :, plane, :],
+                in0=angle[:],
+                in1=gain.unsqueeze(1).to_broadcast([P, TOKEN_TILES, HALF]),
+                op=ALU.mult,
+            )
+
+        def quantise(grouped, codes, scales):
+            nc.vector.quantize_mx(out=codes.bitcast(FP8X4), scales=scales, in_=grouped)
+
+        def quantise_weight(jobs):
+            waiting = None
+            for blocks, matrix, codes, scales in jobs:
+                grouped = weight_stage.tile([P, len(blocks) * K_PASS], BF16, tag="grouped", align_bytes=64)
+                transpose_blocks(nc, psum, grouped[:], matrix, blocks)
+                if waiting is not None:
+                    quantise(*waiting)
+                waiting = (grouped[:], codes, scales)
+            quantise(*waiting)
 
         wd_codes = keep.tile([P, C_PASSES, R_GROUPS, P], U32, name="wd_codes", align_bytes=64)
         wd_scales = keep.tile([P, C_PASSES, R_GROUPS, P], U8, name="wd_scales", align_bytes=64)
-        for first in range(0, C_PASSES, 2):
-            blocks = [
-                wd_raw[t % 2][:, t // 2, g * K_PASS : (g + 1) * K_PASS]
-                for g in range(first, first + 2)
-                for t in range(R_GROUPS)
+        quantise_weight(
+            [
+                (
+                    [
+                        wd_raw[t % 2][:, t // 2, g * K_PASS : (g + 1) * K_PASS]
+                        for g in range(first, first + 2)
+                        for t in range(R_GROUPS)
+                    ],
+                    ident[:],
+                    wd_codes[:, first : first + 2, :, :].rearrange("p g t q -> p (g t q)"),
+                    wd_scales[:, first : first + 2, :, :].rearrange("p g t q -> p (g t q)"),
+                )
+                for first in range(0, C_PASSES, 2)
             ]
-            grouped = weight_stage.tile([P, len(blocks) * K_PASS], BF16, tag="grouped", align_bytes=64)
-            transpose_and_quantise(
-                nc, psum, grouped[:], ident[:], blocks,
-                wd_codes[:, first : first + 2, :, :].rearrange("p g t q -> p (g t q)"),
-                wd_scales[:, first : first + 2, :, :].rearrange("p g t q -> p (g t q)"),
-            )
+        )
 
-        def latent_of_tile(i):
+        x_grouped, x_mx, lat_banks, lat_mx = {}, {}, {}, {}
+
+        def stage_transpose_x(n):
+            x_grouped[n] = token_stage.tile(
+                [P, C_PASSES * K_PASS], BF16, name="x_grouped", tag="x_grouped", align_bytes=64
+            )
+            blocks = [x_raw[n // 2][:, n % 2, g * K_PASS : (g + 1) * K_PASS] for g in range(C_PASSES)]
+            transpose_blocks(nc, psum, x_grouped[n][:], ident[:], blocks)
+
+        def stage_quantise_x(n):
             x_codes = token_stage.tile([P, C_PASSES, P], U32, tag="x_codes", align_bytes=64)
             x_scales = token_stage.tile([P, C_PASSES, P], U8, tag="x_scales", align_bytes=64)
-            x_grouped = token_stage.tile([P, C_PASSES * K_PASS], BF16, tag="x_grouped", align_bytes=64)
-            blocks = [x_raw[i // 2][:, i % 2, g * K_PASS : (g + 1) * K_PASS] for g in range(C_PASSES)]
-            transpose_and_quantise(
-                nc, psum, x_grouped[:], ident[:], blocks,
+            quantise(
+                x_grouped[n][:],
                 x_codes[:].rearrange("p g r -> p (g r)"),
                 x_scales[:].rearrange("p g r -> p (g r)"),
             )
+            x_mx[n] = (x_codes, x_scales)
+
+        def stage_latent(n):
+            x_codes, x_scales = x_mx[n]
             lat_bank = psum.tile([P, R_GROUPS, P], F32, tag="bank")
             for t in range(R_GROUPS):
                 for g in range(C_PASSES):
@@ -163,96 +187,101 @@ def tile_mla_pa_kernel(
                         start=(g == 0),
                         stop=(g == C_PASSES - 1),
                     )
+            lat_banks[n] = lat_bank
+
+        def stage_quantise_latent(n):
             lat_grouped = token_stage.tile([P, P, R_GROUPS], BF16, tag="lat_grouped", align_bytes=64)
-            nc.vector.tensor_copy(out=lat_grouped[:], in_=lat_bank[:].rearrange("p t r -> p r t"))
+            nc.vector.tensor_copy(out=lat_grouped[:], in_=lat_banks[n][:].rearrange("p t r -> p r t"))
             lat_codes = token_stage.tile([P, P], U32, tag="lat_codes", align_bytes=64)
             lat_scales = token_stage.tile([P, P], U8, tag="lat_scales", align_bytes=64)
-            nc.vector.quantize_mx(
-                out=lat_codes[:].bitcast(FP8X4),
-                scales=lat_scales[:],
-                in_=lat_grouped[:].rearrange("p r t -> p (r t)"),
-            )
-            return lat_codes, lat_scales
+            quantise(lat_grouped[:].rearrange("p r t -> p (r t)"), lat_codes[:], lat_scales[:])
+            lat_mx[n] = (lat_codes, lat_scales)
 
-        latent = latent_of_tile(0)
+        stage_transpose_x(0)
+        stage_transpose_x(1)
+        stage_quantise_x(0)
+        stage_quantise_x(1)
+        stage_latent(0)
+        stage_quantise_latent(0)
 
         wu_codes = keep.tile([P, 2 * HEADS * D], U32, name="wu_codes", align_bytes=64)
         wu_scales = keep.tile([P, 2 * HEADS * D], U8, name="wu_scales", align_bytes=64)
-        for chunk in range(WU_CHUNKS):
-            blocks = [wu_raw[chunk][:, n, :] for n in range(BLOCKS_PER_CHUNK)]
-            columns = slice(chunk * BLOCKS_PER_CHUNK * P, (chunk + 1) * BLOCKS_PER_CHUNK * P)
-            grouped = weight_stage.tile([P, len(blocks) * K_PASS], BF16, tag="grouped", align_bytes=64)
-            transpose_and_quantise(
-                nc, psum, grouped[:], ident[:], blocks, wu_codes[:, columns], wu_scales[:, columns]
-            )
+        chunk_columns = BLOCKS_PER_CHUNK * P
+        quantise_weight(
+            [
+                (
+                    [wu_raw[chunk][:, n, :] for n in range(BLOCKS_PER_CHUNK)],
+                    split_pairs[:].rearrange("p e j -> p (e j)") if chunk < WU_CHUNKS // 2 else ident[:],
+                    wu_codes[:, chunk * chunk_columns : (chunk + 1) * chunk_columns],
+                    wu_scales[:, chunk * chunk_columns : (chunk + 1) * chunk_columns],
+                )
+                for chunk in range(WU_CHUNKS)
+            ]
+        )
 
-        def project(bank, lat, first_feature):
-            lat_codes, lat_scales = lat
+        def project(bank, n, first_column):
+            lat_codes, lat_scales = lat_mx[n]
             nc.tensor.matmul_mx(
                 out=bank,
                 lhsT=lat_codes[:].bitcast(FP8X4),
                 lhsT_scale=lat_scales[:],
-                rhs=wu_codes[:, first_feature : first_feature + BANK].bitcast(FP8X4),
-                rhs_scale=wu_scales[:, first_feature : first_feature + BANK],
+                rhs=wu_codes[:, first_column : first_column + BANK].bitcast(FP8X4),
+                rhs_scale=wu_scales[:, first_column : first_column + BANK],
                 start=True,
                 stop=True,
             )
 
-        for i in range(TOKEN_TILES):
-            next_latent = latent_of_tile(i + 1) if i + 1 < TOKEN_TILES else None
+        def project_step(i, step, k_rot, v_sb):
+            k_bank = psum.tile([P, HEADS_PER_BANK, D], F32, tag="bank")
+            project(k_bank[:].rearrange("p h d -> p (h d)"), i, step * BANK)
+            v_bank = psum.tile([P, BANK], F32, tag="bank")
+            project(v_bank[:], i, HEADS * D + step * BANK)
 
-            k_rot = results.tile([P, HEADS, D], F32, tag="k_rot", bufs=3)
-            crossed = results.tile([P, 2, HEADS, D // 2], F32, tag="crossed")
-            v_sb = results.tile([P, HEADS * D], F32, tag="v_sb", bufs=3)
-            for b in range(BANKS_PER_HALF):
-                heads = slice(b * HEADS_PER_BANK, (b + 1) * HEADS_PER_BANK)
-
-                k_bank = psum.tile([P, HEADS_PER_BANK, D // 2, 2], F32, tag="bank")
-                project(k_bank[:].rearrange("p h j e -> p (h j e)"), latent, b * BANK)
-                squares = stats.tile([P, HEADS_PER_BANK, D], BF16, tag="squares", bufs=2)
-                sumsq = stats.tile([P, HEADS_PER_BANK], F32, tag="sumsq")
-                rms = stats.tile([P, HEADS_PER_BANK], F32, tag="rms")
-                rstd = stats.tile([P, HEADS_PER_BANK], F32, tag="rstd")
-                for h in range(HEADS_PER_BANK):
-                    nc.scalar.activation(
-                        out=squares[:, h, :],
-                        in_=k_bank[:, h, :, :].rearrange("p j e -> p (j e)"),
-                        func=ACT.Square,
-                        accum_out=sumsq[:, h : h + 1],
-                    )
-                nc.scalar.activation(out=rms[:], in_=sumsq[:], func=ACT.Sqrt, scale=1.0 / D, bias=EPS)
-                nc.vector.reciprocal(out=rstd[:], in_=rms[:])
-                for h in range(HEADS_PER_BANK):
-                    head = b * HEADS_PER_BANK + h
-                    nc.vector.scalar_tensor_tensor(
-                        out=k_rot[:, head, :],
-                        in0=k_bank[:, h, :, :].rearrange("p j e -> p (j e)"),
-                        scalar=rstd[:, h : h + 1],
-                        in1=own[:, i, :, :].rearrange("p j e -> p (j e)"),
-                        op0=ALU.mult,
-                        op1=ALU.mult,
-                    )
-                    for e in range(2):
-                        nc.vector.scalar_tensor_tensor(
-                            out=crossed[:, e, head, :],
-                            in0=k_bank[:, h, :, 1 - e],
-                            scalar=rstd[:, h : h + 1],
-                            in1=partner[:, i, e, :],
-                            op0=ALU.mult,
-                            op1=ALU.mult,
-                        )
-                k_pairs = k_rot[:, heads, :].rearrange("p h (j e) -> p h j e", e=2)
-                nc.gpsimd.tensor_tensor(
-                    out=k_pairs,
-                    in0=k_pairs,
-                    in1=crossed[:, :, heads, :].rearrange("p e h j -> p h j e"),
-                    op=ALU.add,
+            squares = stats.tile([P, HEADS_PER_BANK, D], BF16, tag="squares", bufs=2)
+            sumsq = stats.tile([P, HEADS_PER_BANK], F32, tag="sumsq")
+            rms = stats.tile([P, HEADS_PER_BANK], F32, tag="rms")
+            rstd = stats.tile([P, HEADS_PER_BANK], F32, tag="rstd")
+            for h in range(HEADS_PER_BANK):
+                nc.scalar.activation(
+                    out=squares[:, h, :],
+                    in_=k_bank[:, h, :],
+                    func=ACT.Square,
+                    accum_out=sumsq[:, h : h + 1],
                 )
+            nc.scalar.activation(out=rms[:], in_=sumsq[:], func=ACT.Sqrt, scale=1.0 / D, bias=EPS)
+            nc.scalar.copy(out=v_sb[:, step * BANK : (step + 1) * BANK], in_=v_bank[:])
 
-                v_bank = psum.tile([P, BANK], F32, tag="bank")
-                project(v_bank[:], latent, HEADS * D + b * BANK)
-                nc.scalar.copy(out=v_sb[:, b * BANK : (b + 1) * BANK], in_=v_bank[:])
+            nc.vector.reciprocal(out=rstd[:], in_=rms[:])
+            products = results.tile([P, HEADS_PER_BANK, 4, HALF], F32, tag="products")
+            for h in range(HEADS_PER_BANK):
+                nc.vector.scalar_tensor_tensor(
+                    out=products[:, h, :, :].rearrange("p (w e) j -> p w (e j)", w=2),
+                    in0=k_bank[:, h, :].unsqueeze(1).to_broadcast([P, 2, D]),
+                    scalar=rstd[:, h : h + 1],
+                    in1=rope_table[:, i, :, :].rearrange("p (w e) j -> p w (e j)", w=2),
+                    op0=ALU.mult,
+                    op1=ALU.mult,
+                )
+            planes = products[:].rearrange("p h (w e) j -> p e h j w", w=2)
+            heads = slice(step * HEADS_PER_BANK, (step + 1) * HEADS_PER_BANK)
+            nc.gpsimd.tensor_tensor(
+                out=k_rot[:, heads, :, :], in0=planes[:, 0], in1=planes[:, 1], op=ALU.add
+            )
 
+        for i in range(TOKEN_TILES):
+            k_rot = results.tile([P, HEADS, HALF, 2], F32, tag="k_rot")
+            v_sb = results.tile([P, HEADS * D], F32, tag="v_sb")
+            project_step(i, 0, k_rot, v_sb)
+            if i + 2 < TOKEN_TILES:
+                stage_transpose_x(i + 2)
+            if i + 1 < TOKEN_TILES:
+                stage_latent(i + 1)
+            project_step(i, 1, k_rot, v_sb)
+            if i + 2 < TOKEN_TILES:
+                stage_quantise_x(i + 2)
+            if i + 1 < TOKEN_TILES:
+                stage_quantise_latent(i + 1)
+            project_step(i, 2, k_rot, v_sb)
+            project_step(i, 3, k_rot, v_sb)
             nc.sync.dma_start(out=v_out_view[:, i, :], in_=v_sb[:])
-            nc.sync.dma_start(out=k_out_view[:, i, :], in_=k_rot[:].rearrange("p h d -> p (h d)"))
-            latent = next_latent
+            nc.sync.dma_start(out=k_out_view[:, i, :], in_=k_rot[:].rearrange("p h j w -> p (h j w)"))

@@ -23,6 +23,7 @@ TOKEN_TILES = TOKENS // P
 C_PASSES = C // K_PASS
 R_GROUPS = R // P
 HEADS_PER_BANK = BANK // D
+STEPS = HEADS * D // BANK
 WU_CHUNKS = 4
 BLOCKS_PER_CHUNK = 2 * HEADS * D // P // WU_CHUNKS
 
@@ -191,7 +192,7 @@ def tile_mla_pa_kernel(
 
         def stage_quantise_latent(n):
             lat_grouped = token_stage.tile([P, P, R_GROUPS], BF16, tag="lat_grouped", align_bytes=64)
-            nc.vector.tensor_copy(out=lat_grouped[:], in_=lat_banks[n][:].rearrange("p t r -> p r t"))
+            nc.scalar.copy(out=lat_grouped[:], in_=lat_banks[n][:].rearrange("p t r -> p r t"))
             lat_codes = token_stage.tile([P, P], U32, tag="lat_codes", align_bytes=64)
             lat_scales = token_stage.tile([P, P], U8, tag="lat_scales", align_bytes=64)
             quantise(lat_grouped[:].rearrange("p r t -> p (r t)"), lat_codes[:], lat_scales[:])
@@ -231,7 +232,18 @@ def tile_mla_pa_kernel(
                 stop=True,
             )
 
-        def project_step(i, step, k_rot, v_sb):
+        def add_planes(i, step, products, k_rot):
+            planes = products[:].rearrange("p h (w e) j -> p e h j w", w=2)
+            heads = slice(step * HEADS_PER_BANK, (step + 1) * HEADS_PER_BANK)
+            nc.vector.tensor_tensor(
+                out=k_rot[:, heads, :, :], in0=planes[:, 0], in1=planes[:, 1], op=ALU.add
+            )
+            if step == STEPS - 1:
+                nc.sync.dma_start(
+                    out=k_out_view[:, i, :], in_=k_rot[:].rearrange("p h j w -> p (h j w)")
+                )
+
+        def project_step(i, step, k_rot, v_sb, unsummed):
             k_bank = psum.tile([P, HEADS_PER_BANK, D], F32, tag="bank")
             project(k_bank[:].rearrange("p h d -> p (h d)"), i, step * BANK)
             v_bank = psum.tile([P, BANK], F32, tag="bank")
@@ -250,6 +262,8 @@ def tile_mla_pa_kernel(
                 )
             nc.scalar.activation(out=rms[:], in_=sumsq[:], func=ACT.Sqrt, scale=1.0 / D, bias=EPS)
             nc.scalar.copy(out=v_sb[:, step * BANK : (step + 1) * BANK], in_=v_bank[:])
+            if step == STEPS - 1:
+                nc.sync.dma_start(out=v_out_view[:, i, :], in_=v_sb[:])
 
             nc.vector.reciprocal(out=rstd[:], in_=rms[:])
             products = results.tile([P, HEADS_PER_BANK, 4, HALF], F32, tag="products")
@@ -262,26 +276,24 @@ def tile_mla_pa_kernel(
                     op0=ALU.mult,
                     op1=ALU.mult,
                 )
-            planes = products[:].rearrange("p h (w e) j -> p e h j w", w=2)
-            heads = slice(step * HEADS_PER_BANK, (step + 1) * HEADS_PER_BANK)
-            nc.gpsimd.tensor_tensor(
-                out=k_rot[:, heads, :, :], in0=planes[:, 0], in1=planes[:, 1], op=ALU.add
-            )
+            if unsummed is not None:
+                add_planes(*unsummed)
+            return (i, step, products, k_rot)
 
+        unsummed = None
         for i in range(TOKEN_TILES):
             k_rot = results.tile([P, HEADS, HALF, 2], F32, tag="k_rot")
             v_sb = results.tile([P, HEADS * D], F32, tag="v_sb")
-            project_step(i, 0, k_rot, v_sb)
+            unsummed = project_step(i, 0, k_rot, v_sb, unsummed)
             if i + 2 < TOKEN_TILES:
                 stage_transpose_x(i + 2)
             if i + 1 < TOKEN_TILES:
                 stage_latent(i + 1)
-            project_step(i, 1, k_rot, v_sb)
+            unsummed = project_step(i, 1, k_rot, v_sb, unsummed)
             if i + 2 < TOKEN_TILES:
                 stage_quantise_x(i + 2)
             if i + 1 < TOKEN_TILES:
                 stage_quantise_latent(i + 1)
-            project_step(i, 2, k_rot, v_sb)
-            project_step(i, 3, k_rot, v_sb)
-            nc.sync.dma_start(out=v_out_view[:, i, :], in_=v_sb[:])
-            nc.sync.dma_start(out=k_out_view[:, i, :], in_=k_rot[:].rearrange("p h j w -> p (h j w)"))
+            unsummed = project_step(i, 2, k_rot, v_sb, unsummed)
+            unsummed = project_step(i, 3, k_rot, v_sb, unsummed)
+        add_planes(*unsummed)

@@ -105,22 +105,22 @@ def tile_mla_pa_kernel(
         split_pairs = keep.tile([P, 2, HALF], F32, name="split_pairs")
         nc.vector.tensor_copy(out=split_pairs[:], in_=ident[:].rearrange("p (j e) -> p e j", e=2))
 
-        rope_table = keep.tile([P, TOKEN_TILES, 4, HALF], F32, name="rope_table")
+        rope_table = keep.tile([P, TOKEN_TILES, 2, HALF, 2], F32, name="rope_table")
         neg_gain = keep.tile([P, HALF, 2], BF16, name="neg_gain")
         nc.gpsimd.tensor_scalar(
             out=neg_gain[:], in0=gain_bf[:], scalar1=-1.0, scalar2=0.0, op0=ALU.mult, op1=ALU.add
         )
-        plane_factors = [
-            (cos_bf, gain_bf[:, :, 0]),
-            (sin_bf, neg_gain[:, :, 1]),
-            (sin_bf, gain_bf[:, :, 0]),
-            (cos_bf, gain_bf[:, :, 1]),
+        factors = [
+            (0, 0, cos_bf, gain_bf),
+            (0, 1, sin_bf, gain_bf),
+            (1, 0, sin_bf, neg_gain),
+            (1, 1, cos_bf, gain_bf),
         ]
-        for plane, (angle, gain) in enumerate(plane_factors):
+        for e, w, angle, gain in factors:
             nc.gpsimd.tensor_tensor(
-                out=rope_table[:, :, plane, :],
+                out=rope_table[:, :, e, :, w],
                 in0=angle[:],
-                in1=gain.unsqueeze(1).to_broadcast([P, TOKEN_TILES, HALF]),
+                in1=gain[:, :, e].unsqueeze(1).to_broadcast([P, TOKEN_TILES, HALF]),
                 op=ALU.mult,
             )
 
@@ -232,18 +232,15 @@ def tile_mla_pa_kernel(
                 stop=True,
             )
 
-        def add_planes(i, step, products, k_rot):
-            planes = products[:].rearrange("p h (w e) j -> p e h j w", w=2)
+        def add_products(i, step, products, k_rot):
             heads = slice(step * HEADS_PER_BANK, (step + 1) * HEADS_PER_BANK)
-            nc.vector.tensor_tensor(
-                out=k_rot[:, heads, :, :], in0=planes[:, 0], in1=planes[:, 1], op=ALU.add
+            nc.gpsimd.tensor_tensor(
+                out=k_rot[:, heads, :], in0=products[:, :, 0, :], in1=products[:, :, 1, :], op=ALU.add
             )
             if step == STEPS - 1:
-                nc.sync.dma_start(
-                    out=k_out_view[:, i, :], in_=k_rot[:].rearrange("p h j w -> p (h j w)")
-                )
+                nc.sync.dma_start(out=k_out_view[:, i, :], in_=k_rot[:].rearrange("p h d -> p (h d)"))
 
-        def project_step(i, step, k_rot, v_sb, unsummed):
+        def project_step(i, step, k_rot, v_sb):
             k_bank = psum.tile([P, HEADS_PER_BANK, D], F32, tag="bank")
             project(k_bank[:].rearrange("p h d -> p (h d)"), i, step * BANK)
             v_bank = psum.tile([P, BANK], F32, tag="bank")
@@ -266,34 +263,30 @@ def tile_mla_pa_kernel(
                 nc.sync.dma_start(out=v_out_view[:, i, :], in_=v_sb[:])
 
             nc.vector.reciprocal(out=rstd[:], in_=rms[:])
-            products = results.tile([P, HEADS_PER_BANK, 4, HALF], F32, tag="products")
+            products = results.tile([P, HEADS_PER_BANK, 2, D], F32, tag="products", bufs=4)
             for h in range(HEADS_PER_BANK):
                 nc.vector.scalar_tensor_tensor(
-                    out=products[:, h, :, :].rearrange("p (w e) j -> p w (e j)", w=2),
-                    in0=k_bank[:, h, :].unsqueeze(1).to_broadcast([P, 2, D]),
+                    out=products[:, h, :, :].rearrange("p e (j w) -> p (e j) w", w=2),
+                    in0=k_bank[:, h, :].unsqueeze(2).to_broadcast([P, D, 2]),
                     scalar=rstd[:, h : h + 1],
-                    in1=rope_table[:, i, :, :].rearrange("p (w e) j -> p w (e j)", w=2),
+                    in1=rope_table[:, i, :, :, :].rearrange("p e j w -> p (e j) w"),
                     op0=ALU.mult,
                     op1=ALU.mult,
                 )
-            if unsummed is not None:
-                add_planes(*unsummed)
-            return (i, step, products, k_rot)
+            add_products(i, step, products, k_rot)
 
-        unsummed = None
         for i in range(TOKEN_TILES):
-            k_rot = results.tile([P, HEADS, HALF, 2], F32, tag="k_rot")
+            k_rot = results.tile([P, HEADS, D], F32, tag="k_rot")
             v_sb = results.tile([P, HEADS * D], F32, tag="v_sb")
-            unsummed = project_step(i, 0, k_rot, v_sb, unsummed)
+            project_step(i, 0, k_rot, v_sb)
             if i + 2 < TOKEN_TILES:
                 stage_transpose_x(i + 2)
             if i + 1 < TOKEN_TILES:
                 stage_latent(i + 1)
-            unsummed = project_step(i, 1, k_rot, v_sb, unsummed)
+            project_step(i, 1, k_rot, v_sb)
             if i + 2 < TOKEN_TILES:
                 stage_quantise_x(i + 2)
             if i + 1 < TOKEN_TILES:
                 stage_quantise_latent(i + 1)
-            unsummed = project_step(i, 2, k_rot, v_sb, unsummed)
-            unsummed = project_step(i, 3, k_rot, v_sb, unsummed)
-        add_planes(*unsummed)
+            project_step(i, 2, k_rot, v_sb)
+            project_step(i, 3, k_rot, v_sb)

@@ -23,7 +23,6 @@ TOKEN_TILES = TOKENS // P
 C_PASSES = C // K_PASS
 R_GROUPS = R // P
 HEADS_PER_BANK = BANK // D
-STEPS = HEADS * D // BANK
 WU_CHUNKS = 4
 BLOCKS_PER_CHUNK = 2 * HEADS * D // P // WU_CHUNKS
 
@@ -99,7 +98,7 @@ def tile_mla_pa_kernel(
 
         one = keep.tile([P, 1], F32, name="one")
         nc.vector.memset(one[:], 1.0)
-        nc.scalar.activation(out=one[:], in_=one[:], func=ACT.Sqrt)
+        nc.scalar.activation(out=one[:], in_=one[:], func=ACT.Abs_reciprocal_sqrt)
         ident = keep.tile([P, P], F32, name="ident")
         make_identity(nc, ident[:])
         split_pairs = keep.tile([P, 2, HALF], F32, name="split_pairs")
@@ -232,13 +231,17 @@ def tile_mla_pa_kernel(
                 stop=True,
             )
 
+        def store_two_banks(out_view, i, step, result):
+            columns = slice((step - 1) * BANK, (step + 1) * BANK)
+            nc.sync.dma_start(out=out_view[:, i, columns], in_=result[:, columns])
+
         def add_products(i, step, products, k_rot):
             heads = slice(step * HEADS_PER_BANK, (step + 1) * HEADS_PER_BANK)
             nc.gpsimd.tensor_tensor(
                 out=k_rot[:, heads, :], in0=products[:, :, 0, :], in1=products[:, :, 1, :], op=ALU.add
             )
-            if step == STEPS - 1:
-                nc.sync.dma_start(out=k_out_view[:, i, :], in_=k_rot[:].rearrange("p h d -> p (h d)"))
+            if step % 2 == 1:
+                store_two_banks(k_out_view, i, step, k_rot[:].rearrange("p h d -> p (h d)"))
 
         def project_step(i, step, k_rot, v_sb):
             k_bank = psum.tile([P, HEADS_PER_BANK, D], F32, tag="bank")
@@ -248,7 +251,6 @@ def tile_mla_pa_kernel(
 
             squares = stats.tile([P, HEADS_PER_BANK, D], BF16, tag="squares", bufs=2)
             sumsq = stats.tile([P, HEADS_PER_BANK], F32, tag="sumsq")
-            rms = stats.tile([P, HEADS_PER_BANK], F32, tag="rms")
             rstd = stats.tile([P, HEADS_PER_BANK], F32, tag="rstd")
             for h in range(HEADS_PER_BANK):
                 nc.scalar.activation(
@@ -257,12 +259,13 @@ def tile_mla_pa_kernel(
                     func=ACT.Square,
                     accum_out=sumsq[:, h : h + 1],
                 )
-            nc.scalar.activation(out=rms[:], in_=sumsq[:], func=ACT.Sqrt, scale=1.0 / D, bias=EPS)
             nc.scalar.copy(out=v_sb[:, step * BANK : (step + 1) * BANK], in_=v_bank[:])
-            if step == STEPS - 1:
-                nc.sync.dma_start(out=v_out_view[:, i, :], in_=v_sb[:])
+            if step % 2 == 1:
+                store_two_banks(v_out_view, i, step, v_sb[:])
+            nc.scalar.activation(
+                out=rstd[:], in_=sumsq[:], func=ACT.Abs_reciprocal_sqrt, scale=1.0 / D, bias=EPS
+            )
 
-            nc.vector.reciprocal(out=rstd[:], in_=rms[:])
             products = results.tile([P, HEADS_PER_BANK, 2, D], F32, tag="products", bufs=4)
             for h in range(HEADS_PER_BANK):
                 nc.vector.scalar_tensor_tensor(

@@ -23,6 +23,7 @@ TOKEN_TILES = TOKENS // P
 C_PASSES = C // K_PASS
 R_GROUPS = R // P
 HEADS_PER_BANK = BANK // D
+VECTOR_VALUES_STEP = 2
 WU_CHUNKS = 4
 BLOCKS_PER_CHUNK = 2 * HEADS * D // P // WU_CHUNKS
 
@@ -154,7 +155,7 @@ def tile_mla_pa_kernel(
             ]
         )
 
-        x_grouped, x_mx, lat_banks, lat_mx = {}, {}, {}, {}
+        x_grouped, x_mx, lat_banks, lat_grouped, lat_mx = {}, {}, {}, {}, {}
 
         def stage_transpose_x(n):
             x_grouped[n] = token_stage.tile(
@@ -189,12 +190,16 @@ def tile_mla_pa_kernel(
                     )
             lat_banks[n] = lat_bank
 
+        def stage_round_latent(n):
+            lat_grouped[n] = token_stage.tile(
+                [P, P, R_GROUPS], BF16, name="lat_grouped", tag="lat_grouped", align_bytes=64
+            )
+            nc.vector.tensor_copy(out=lat_grouped[n][:], in_=lat_banks[n][:].rearrange("p t r -> p r t"))
+
         def stage_quantise_latent(n):
-            lat_grouped = token_stage.tile([P, P, R_GROUPS], BF16, tag="lat_grouped", align_bytes=64)
-            nc.scalar.copy(out=lat_grouped[:], in_=lat_banks[n][:].rearrange("p t r -> p r t"))
             lat_codes = token_stage.tile([P, P], U32, tag="lat_codes", align_bytes=64)
             lat_scales = token_stage.tile([P, P], U8, tag="lat_scales", align_bytes=64)
-            quantise(lat_grouped[:].rearrange("p r t -> p (r t)"), lat_codes[:], lat_scales[:])
+            quantise(lat_grouped[n][:].rearrange("p r t -> p (r t)"), lat_codes[:], lat_scales[:])
             lat_mx[n] = (lat_codes, lat_scales)
 
         stage_transpose_x(0)
@@ -202,6 +207,7 @@ def tile_mla_pa_kernel(
         stage_quantise_x(0)
         stage_quantise_x(1)
         stage_latent(0)
+        stage_round_latent(0)
         stage_quantise_latent(0)
 
         wu_codes = keep.tile([P, 2 * HEADS * D], U32, name="wu_codes", align_bytes=64)
@@ -259,9 +265,8 @@ def tile_mla_pa_kernel(
                     func=ACT.Square,
                     accum_out=sumsq[:, h : h + 1],
                 )
-            nc.scalar.copy(out=v_sb[:, step * BANK : (step + 1) * BANK], in_=v_bank[:])
-            if step % 2 == 1:
-                store_two_banks(v_out_view, i, step, v_sb[:])
+            if step != VECTOR_VALUES_STEP:
+                nc.scalar.copy(out=v_sb[:, step * BANK : (step + 1) * BANK], in_=v_bank[:])
             nc.scalar.activation(
                 out=rstd[:], in_=sumsq[:], func=ACT.Abs_reciprocal_sqrt, scale=1.0 / D, bias=EPS
             )
@@ -277,6 +282,10 @@ def tile_mla_pa_kernel(
                     op1=ALU.mult,
                 )
             add_products(i, step, products, k_rot)
+            if step == VECTOR_VALUES_STEP:
+                nc.vector.tensor_copy(out=v_sb[:, step * BANK : (step + 1) * BANK], in_=v_bank[:])
+            if step % 2 == 1:
+                store_two_banks(v_out_view, i, step, v_sb[:])
 
         for i in range(TOKEN_TILES):
             k_rot = results.tile([P, HEADS, D], F32, tag="k_rot")
@@ -286,10 +295,12 @@ def tile_mla_pa_kernel(
                 stage_transpose_x(i + 2)
             if i + 1 < TOKEN_TILES:
                 stage_latent(i + 1)
-            project_step(i, 1, k_rot, v_sb)
+            if i + 1 < TOKEN_TILES:
+                stage_round_latent(i + 1)
             if i + 2 < TOKEN_TILES:
                 stage_quantise_x(i + 2)
             if i + 1 < TOKEN_TILES:
                 stage_quantise_latent(i + 1)
+            project_step(i, 1, k_rot, v_sb)
             project_step(i, 2, k_rot, v_sb)
             project_step(i, 3, k_rot, v_sb)

@@ -207,7 +207,9 @@ def tile_mla_pa_kernel(
         stage_quantise_x(0)
         stage_quantise_x(1)
         stage_latent(0)
+        stage_latent(1)
         stage_round_latent(0)
+        stage_round_latent(1)
         stage_quantise_latent(0)
 
         wu_codes = keep.tile([P, 2 * HEADS * D], U32, name="wu_codes", align_bytes=64)
@@ -293,14 +295,12 @@ def tile_mla_pa_kernel(
             project_step(i, 0, k_rot, v_sb)
             if i + 2 < TOKEN_TILES:
                 stage_transpose_x(i + 2)
-            if i + 1 < TOKEN_TILES:
-                stage_latent(i + 1)
-            if i + 1 < TOKEN_TILES:
-                stage_round_latent(i + 1)
-            if i + 2 < TOKEN_TILES:
                 stage_quantise_x(i + 2)
             if i + 1 < TOKEN_TILES:
                 stage_quantise_latent(i + 1)
             project_step(i, 1, k_rot, v_sb)
             project_step(i, 2, k_rot, v_sb)
             project_step(i, 3, k_rot, v_sb)
+            if i + 2 < TOKEN_TILES:
+                stage_latent(i + 2)
+                stage_round_latent(i + 2)

@@ -24,8 +24,9 @@ C_PASSES = C // K_PASS
 R_GROUPS = R // P
 HEADS_PER_BANK = BANK // D
 VECTOR_VALUES_STEP = 2
-WU_CHUNKS = 4
-BLOCKS_PER_CHUNK = 2 * HEADS * D // P // WU_CHUNKS
+KEYS, VALUES = 0, 1
+BLOCKS_PER_CHUNK = HEADS * D // 2 // P
+BANKS_PER_CHUNK = BLOCKS_PER_CHUNK * P // BANK
 
 FLOPS = 2 * TOKENS * C * R + 2 * TOKENS * R * 2 * HEADS * D
 
@@ -77,14 +78,15 @@ def tile_mla_pa_kernel(
             x_raw.append(keep.tile([P, 2, C], BF16, name="x_raw%d" % pair))
         nc.sync.dma_start(out=x_raw[0][:], in_=x_view[:, 0:2, :])
         wu_blocks = w_kv_up.rearrange("(n p) r -> p n r", p=P)
-        wu_raw = []
-        for chunk in range(WU_CHUNKS):
-            wu_part = keep.tile([P, BLOCKS_PER_CHUNK, R], BF16, name="wu_raw%d" % chunk)
-            nc.sync.dma_start(
-                out=wu_part[:],
-                in_=wu_blocks[:, chunk * BLOCKS_PER_CHUNK : (chunk + 1) * BLOCKS_PER_CHUNK, :],
-            )
-            wu_raw.append(wu_part)
+        wu_raw = {}
+        for half in range(2):
+            for kind in (KEYS, VALUES):
+                first_block = (2 * kind + half) * BLOCKS_PER_CHUNK
+                wu_part = keep.tile([P, BLOCKS_PER_CHUNK, R], BF16, name="wu_raw%d%d" % (kind, half))
+                nc.sync.dma_start(
+                    out=wu_part[:], in_=wu_blocks[:, first_block : first_block + BLOCKS_PER_CHUNK, :]
+                )
+                wu_raw[(kind, half)] = wu_part
         for pair in range(1, TOKEN_TILES // 2):
             nc.sync.dma_start(out=x_raw[pair][:], in_=x_view[:, 2 * pair : 2 * pair + 2, :])
 
@@ -127,33 +129,43 @@ def tile_mla_pa_kernel(
         def quantise(grouped, codes, scales):
             nc.vector.quantize_mx(out=codes.bitcast(FP8X4), scales=scales, in_=grouped)
 
-        def quantise_weight(jobs):
-            waiting = None
-            for blocks, matrix, codes, scales in jobs:
-                grouped = weight_stage.tile([P, len(blocks) * K_PASS], BF16, tag="grouped", align_bytes=64)
-                transpose_blocks(nc, psum, grouped[:], matrix, blocks)
-                if waiting is not None:
-                    quantise(*waiting)
-                waiting = (grouped[:], codes, scales)
-            quantise(*waiting)
+        def transpose_weight(blocks, matrix):
+            grouped = weight_stage.tile([P, len(blocks) * K_PASS], BF16, tag="grouped", align_bytes=64)
+            transpose_blocks(nc, psum, grouped[:], matrix, blocks)
+            return grouped
 
         wd_codes = keep.tile([P, C_PASSES, R_GROUPS, P], U32, name="wd_codes", align_bytes=64)
         wd_scales = keep.tile([P, C_PASSES, R_GROUPS, P], U8, name="wd_scales", align_bytes=64)
-        quantise_weight(
-            [
-                (
-                    [
-                        wd_raw[t % 2][:, t // 2, g * K_PASS : (g + 1) * K_PASS]
-                        for g in range(first, first + 2)
-                        for t in range(R_GROUPS)
-                    ],
-                    ident[:],
-                    wd_codes[:, first : first + 2, :, :].rearrange("p g t q -> p (g t q)"),
-                    wd_scales[:, first : first + 2, :, :].rearrange("p g t q -> p (g t q)"),
-                )
-                for first in range(0, C_PASSES, 2)
+
+        def transpose_wd(first_pass):
+            blocks = [
+                wd_raw[t % 2][:, t // 2, g * K_PASS : (g + 1) * K_PASS]
+                for g in range(first_pass, first_pass + 2)
+                for t in range(R_GROUPS)
             ]
-        )
+            return transpose_weight(blocks, ident[:])
+
+        def quantise_wd(first_pass, grouped):
+            passes = slice(first_pass, first_pass + 2)
+            quantise(
+                grouped[:],
+                wd_codes[:, passes, :, :].rearrange("p g t q -> p (g t q)"),
+                wd_scales[:, passes, :, :].rearrange("p g t q -> p (g t q)"),
+            )
+
+        wu_mx = {}
+
+        def transpose_wu(kind, half):
+            blocks = [wu_raw[(kind, half)][:, n, :] for n in range(BLOCKS_PER_CHUNK)]
+            matrix = split_pairs[:].rearrange("p e j -> p (e j)") if kind == KEYS else ident[:]
+            return transpose_weight(blocks, matrix)
+
+        def quantise_wu(kind, half, grouped):
+            columns = BLOCKS_PER_CHUNK * P
+            wu_codes = keep.tile([P, columns], U32, name="wu_codes%d%d" % (kind, half), align_bytes=64)
+            wu_scales = keep.tile([P, columns], U8, name="wu_scales%d%d" % (kind, half), align_bytes=64)
+            quantise(grouped[:], wu_codes[:], wu_scales[:])
+            wu_mx[(kind, half)] = (wu_codes, wu_scales)
 
         x_grouped, x_mx, lat_banks, lat_grouped, lat_mx = {}, {}, {}, {}, {}
 
@@ -202,39 +214,38 @@ def tile_mla_pa_kernel(
             quantise(lat_grouped[n][:].rearrange("p r t -> p (r t)"), lat_codes[:], lat_scales[:])
             lat_mx[n] = (lat_codes, lat_scales)
 
+        wd_first = transpose_wd(0)
+        wd_second = transpose_wd(2)
+        quantise_wd(0, wd_first)
         stage_transpose_x(0)
         stage_transpose_x(1)
+        quantise_wd(2, wd_second)
+        keys_low = transpose_wu(KEYS, 0)
         stage_quantise_x(0)
         stage_quantise_x(1)
+        values_low = transpose_wu(VALUES, 0)
+        quantise_wu(KEYS, 0, keys_low)
         stage_latent(0)
         stage_latent(1)
+        quantise_wu(VALUES, 0, values_low)
         stage_round_latent(0)
         stage_round_latent(1)
         stage_quantise_latent(0)
+        keys_high = transpose_wu(KEYS, 1)
+        values_high = transpose_wu(VALUES, 1)
+        quantise_wu(KEYS, 1, keys_high)
+        quantise_wu(VALUES, 1, values_high)
 
-        wu_codes = keep.tile([P, 2 * HEADS * D], U32, name="wu_codes", align_bytes=64)
-        wu_scales = keep.tile([P, 2 * HEADS * D], U8, name="wu_scales", align_bytes=64)
-        chunk_columns = BLOCKS_PER_CHUNK * P
-        quantise_weight(
-            [
-                (
-                    [wu_raw[chunk][:, n, :] for n in range(BLOCKS_PER_CHUNK)],
-                    split_pairs[:].rearrange("p e j -> p (e j)") if chunk < WU_CHUNKS // 2 else ident[:],
-                    wu_codes[:, chunk * chunk_columns : (chunk + 1) * chunk_columns],
-                    wu_scales[:, chunk * chunk_columns : (chunk + 1) * chunk_columns],
-                )
-                for chunk in range(WU_CHUNKS)
-            ]
-        )
-
-        def project(bank, n, first_column):
+        def project(bank, n, kind, step):
             lat_codes, lat_scales = lat_mx[n]
+            wu_codes, wu_scales = wu_mx[(kind, step // BANKS_PER_CHUNK)]
+            columns = slice((step % BANKS_PER_CHUNK) * BANK, (step % BANKS_PER_CHUNK + 1) * BANK)
             nc.tensor.matmul_mx(
                 out=bank,
                 lhsT=lat_codes[:].bitcast(FP8X4),
                 lhsT_scale=lat_scales[:],
-                rhs=wu_codes[:, first_column : first_column + BANK].bitcast(FP8X4),
-                rhs_scale=wu_scales[:, first_column : first_column + BANK],
+                rhs=wu_codes[:, columns].bitcast(FP8X4),
+                rhs_scale=wu_scales[:, columns],
                 start=True,
                 stop=True,
             )
@@ -253,9 +264,9 @@ def tile_mla_pa_kernel(
 
         def project_step(i, step, k_rot, v_sb):
             k_bank = psum.tile([P, HEADS_PER_BANK, D], F32, tag="bank")
-            project(k_bank[:].rearrange("p h d -> p (h d)"), i, step * BANK)
+            project(k_bank[:].rearrange("p h d -> p (h d)"), i, KEYS, step)
             v_bank = psum.tile([P, BANK], F32, tag="bank")
-            project(v_bank[:], i, HEADS * D + step * BANK)
+            project(v_bank[:], i, VALUES, step)
 
             squares = stats.tile([P, HEADS_PER_BANK, D], BF16, tag="squares", bufs=2)
             sumsq = stats.tile([P, HEADS_PER_BANK], F32, tag="sumsq")

from contextlib import ExitStack

import concourse.mybir as mybir
from concourse.masks import make_identity

F32 = mybir.dt.float32
BF16 = mybir.dt.bfloat16
U32 = mybir.dt.uint32
U8 = mybir.dt.uint8
FP8X4 = mybir.dt.float8_e4m3fn_x4
ALU = mybir.AluOpType
ACT = mybir.ActivationFunctionType

P = 128
PACK = 4
K_PASS = P * PACK
BANK = 512

TOKENS, C, R, HEADS, D = 1024, 2048, 512, 16, 128
EPS = 1e-6
HALF = D // 2
TOKEN_TILES = TOKENS // P
C_PASSES = C // K_PASS
R_GROUPS = R // P
HEADS_PER_BANK = BANK // D
VECTOR_VALUES_STEP = 2
KEYS, VALUES = 0, 1
BLOCKS_PER_CHUNK = HEADS * D // 2 // P
BANKS_PER_CHUNK = BLOCKS_PER_CHUNK * P // BANK

FLOPS = 2 * TOKENS * C * R + 2 * TOKENS * R * 2 * HEADS * D


def transpose_blocks(nc, psum, grouped, matrix, blocks):
    grouped_words = grouped.bitcast(F32).rearrange("p (a r u) -> p a r u", r=P, u=2)
    for pair in range(len(blocks) // 2):
        bank = psum.tile([P, 2, 2, P], F32, tag="bank")
        for a in range(2):
            words = blocks[2 * pair + a].bitcast(F32)
            for u in range(2):
                nc.tensor.transpose(bank[:, a, u, :], words[:, u * P : (u + 1) * P], matrix)
        copy_out = nc.vector.tensor_copy if pair % 4 == 3 else nc.scalar.copy
        copy_out(
            out=grouped_words[:, 2 * pair : 2 * pair + 2, :, :],
            in_=bank[:].rearrange("p a u r -> p a r u"),
        )


def tile_mla_pa_kernel(
    tc, x, w_kv_down, w_kv_up, k_norm_w, freqs_cos, freqs_sin, out_0, out_1
):
    nc = tc.nc
    x_view = x.flatten_outer_dims().rearrange("(p i) c -> p i c", i=TOKEN_TILES)
    k_out_view = out_0.flatten_outer_dims().rearrange(
        "(p i h) d -> p i (h d)", i=TOKEN_TILES, h=HEADS
    )
    v_out_view = out_1.flatten_outer_dims().rearrange(
        "(p i h) d -> p i (h d)", i=TOKEN_TILES, h=HEADS
    )

    with ExitStack() as stack:
        stack.enter_context(tc.manual_schedule())
        keep = stack.enter_context(tc.tile_pool(name="keep", bufs=1))
        weight_stage = stack.enter_context(tc.tile_pool(name="weight_stage", bufs=3))
        token_stage = stack.enter_context(tc.tile_pool(name="token_stage", bufs=2))
        stats = stack.enter_context(tc.tile_pool(name="stats", bufs=4))
        results = stack.enter_context(tc.tile_pool(name="results", bufs=3))
        psum = stack.enter_context(tc.psum_pool(name="psum", bufs=8))

        wd_rows = w_kv_down.rearrange("(u q e) c -> e q u c", u=2, e=2)
        wd_raw = []
        for e in range(2):
            wd_half = keep.tile([P, 2, C], BF16, name="wd_raw%d" % e)
            nc.sync.dma_start(out=wd_half[:], in_=wd_rows[e])
            wd_raw.append(wd_half)
        x_raw = []
        for pair in range(TOKEN_TILES // 2):
            x_raw.append(keep.tile([P, 2, C], BF16, name="x_raw%d" % pair))
        nc.sync.dma_start(out=x_raw[0][:], in_=x_view[:, 0:2, :])
        wu_blocks = w_kv_up.rearrange("(n p) r -> p n r", p=P)
        wu_raw = {}
        for half in range(2):
            for kind in (KEYS, VALUES):
                first_block = (2 * kind + half) * BLOCKS_PER_CHUNK
                wu_part = keep.tile([P, BLOCKS_PER_CHUNK, R], BF16, name="wu_raw%d%d" % (kind, half))
                nc.sync.dma_start(
                    out=wu_part[:], in_=wu_blocks[:, first_block : first_block + BLOCKS_PER_CHUNK, :]
                )
                wu_raw[(kind, half)] = wu_part
        for pair in range(1, TOKEN_TILES // 2):
            nc.sync.dma_start(out=x_raw[pair][:], in_=x_view[:, 2 * pair : 2 * pair + 2, :])

        cos_bf = keep.tile([P, TOKEN_TILES, HALF], BF16, name="cos_bf")
        sin_bf = keep.tile([P, TOKEN_TILES, HALF], BF16, name="sin_bf")
        gain_bf = keep.tile([P, HALF, 2], BF16, name="gain_bf")
        nc.scalar.dma_start(out=cos_bf[:], in_=freqs_cos.rearrange("(p i) j -> p i j", i=TOKEN_TILES))
        nc.scalar.dma_start(out=sin_bf[:], in_=freqs_sin.rearrange("(p i) j -> p i j", i=TOKEN_TILES))
        nc.scalar.dma_start(
            out=gain_bf[:].rearrange("p j e -> p (j e)"), in_=k_norm_w.partition_broadcast(P)
        )

        one = keep.tile([P, 1], F32, name="one")
        nc.vector.memset(one[:], 1.0)
        nc.scalar.activation(out=one[:], in_=one[:], func=ACT.Abs_reciprocal_sqrt)
        ident = keep.tile([P, P], F32, name="ident")
        make_identity(nc, ident[:])
        split_pairs = keep.tile([P, 2, HALF], F32, name="split_pairs")
        nc.vector.tensor_copy(out=split_pairs[:], in_=ident[:].rearrange("p (j e) -> p e j", e=2))

        rope_table = keep.tile([P, TOKEN_TILES, 2, HALF, 2], F32, name="rope_table")
        neg_gain = keep.tile([P, HALF, 2], BF16, name="neg_gain")
        nc.gpsimd.tensor_scalar(
            out=neg_gain[:], in0=gain_bf[:], scalar1=-1.0, scalar2=0.0, op0=ALU.mult, op1=ALU.add
        )
        factors = [
            (0, 0, cos_bf, gain_bf),
            (0, 1, sin_bf, gain_bf),
            (1, 0, sin_bf, neg_gain),
            (1, 1, cos_bf, gain_bf),
        ]
        for e, w, angle, gain in factors:
            nc.gpsimd.tensor_tensor(
                out=rope_table[:, :, e, :, w],
                in0=angle[:],
                in1=gain[:, :, e].unsqueeze(1).to_broadcast([P, TOKEN_TILES, HALF]),
                op=ALU.mult,
            )

        def quantise(grouped, codes, scales):
            nc.vector.quantize_mx(out=codes.bitcast(FP8X4), scales=scales, in_=grouped)

        def transpose_weight(blocks, matrix):
            grouped = weight_stage.tile([P, len(blocks) * K_PASS], BF16, tag="grouped", align_bytes=64)
            transpose_blocks(nc, psum, grouped[:], matrix, blocks)
            return grouped

        wd_codes = keep.tile([P, C_PASSES, R_GROUPS, P], U32, name="wd_codes", align_bytes=64)
        wd_scales = keep.tile([P, C_PASSES, R_GROUPS, P], U8, name="wd_scales", align_bytes=64)

        def transpose_wd(first_pass):
            blocks = [
                wd_raw[t % 2][:, t // 2, g * K_PASS : (g + 1) * K_PASS]
                for g in range(first_pass, first_pass + 2)
                for t in range(R_GROUPS)
            ]
            return transpose_weight(blocks, ident[:])

        def quantise_wd(first_pass, grouped):
            passes = slice(first_pass, first_pass + 2)
            quantise(
                grouped[:],
                wd_codes[:, passes, :, :].rearrange("p g t q -> p (g t q)"),
                wd_scales[:, passes, :, :].rearrange("p g t q -> p (g t q)"),
            )

        wu_mx = {}

        def transpose_wu(kind, half):
            blocks = [wu_raw[(kind, half)][:, n, :] for n in range(BLOCKS_PER_CHUNK)]
            matrix = split_pairs[:].rearrange("p e j -> p (e j)") if kind == KEYS else ident[:]
            return transpose_weight(blocks, matrix)

        def quantise_wu(kind, half, grouped):
            columns = BLOCKS_PER_CHUNK * P
            wu_codes = keep.tile([P, columns], U32, name="wu_codes%d%d" % (kind, half), align_bytes=64)
            wu_scales = keep.tile([P, columns], U8, name="wu_scales%d%d" % (kind, half), align_bytes=64)
            quantise(grouped[:], wu_codes[:], wu_scales[:])
            wu_mx[(kind, half)] = (wu_codes, wu_scales)

        x_grouped, x_mx, lat_banks, lat_grouped, lat_mx = {}, {}, {}, {}, {}

        def stage_transpose_x(n):
            x_grouped[n] = token_stage.tile(
                [P, C_PASSES * K_PASS], BF16, name="x_grouped", tag="x_grouped", align_bytes=64
            )
            blocks = [x_raw[n // 2][:, n % 2, g * K_PASS : (g + 1) * K_PASS] for g in range(C_PASSES)]
            transpose_blocks(nc, psum, x_grouped[n][:], ident[:], blocks)

        def stage_quantise_x(n):
            x_codes = token_stage.tile([P, C_PASSES, P], U32, tag="x_codes", align_bytes=64)
            x_scales = token_stage.tile([P, C_PASSES, P], U8, tag="x_scales", align_bytes=64)
            quantise(
                x_grouped[n][:],
                x_codes[:].rearrange("p g r -> p (g r)"),
                x_scales[:].rearrange("p g r -> p (g r)"),
            )
            x_mx[n] = (x_codes, x_scales)

        def stage_latent(n):
            x_codes, x_scales = x_mx[n]
            lat_bank = psum.tile([P, R_GROUPS, P], F32, tag="bank")
            for t in range(R_GROUPS):
                for g in range(C_PASSES):
                    nc.tensor.matmul_mx(
                        out=lat_bank[:, t, :],
                        lhsT=wd_codes[:, g, t, :].bitcast(FP8X4),
                        lhsT_scale=wd_scales[:, g, t, :],
                        rhs=x_codes[:, g, :].bitcast(FP8X4),
                        rhs_scale=x_scales[:, g, :],
                        start=(g == 0),
                        stop=(g == C_PASSES - 1),
                    )
            lat_banks[n] = lat_bank

        def stage_round_latent(n):
            lat_grouped[n] = token_stage.tile(
                [P, P, R_GROUPS], BF16, name="lat_grouped", tag="lat_grouped", align_bytes=64
            )
            nc.vector.tensor_copy(out=lat_grouped[n][:], in_=lat_banks[n][:].rearrange("p t r -> p r t"))

        def stage_quantise_latent(n):
            lat_codes = token_stage.tile([P, P], U32, tag="lat_codes", align_bytes=64)
            lat_scales = token_stage.tile([P, P], U8, tag="lat_scales", align_bytes=64)
            quantise(lat_grouped[n][:].rearrange("p r t -> p (r t)"), lat_codes[:], lat_scales[:])
            lat_mx[n] = (lat_codes, lat_scales)

        wd_first = transpose_wd(0)
        wd_second = transpose_wd(2)
        quantise_wd(0, wd_first)
        stage_transpose_x(0)
        stage_transpose_x(1)
        quantise_wd(2, wd_second)
        keys_low = transpose_wu(KEYS, 0)
        stage_quantise_x(0)
        stage_quantise_x(1)
        values_low = transpose_wu(VALUES, 0)
        quantise_wu(KEYS, 0, keys_low)
        stage_latent(0)
        stage_latent(1)
        quantise_wu(VALUES, 0, values_low)
        stage_round_latent(0)
        stage_round_latent(1)
        stage_quantise_latent(0)
        keys_high = transpose_wu(KEYS, 1)
        values_high = transpose_wu(VALUES, 1)
        quantise_wu(KEYS, 1, keys_high)
        quantise_wu(VALUES, 1, values_high)

        def project(bank, n, kind, step):
            lat_codes, lat_scales = lat_mx[n]
            wu_codes, wu_scales = wu_mx[(kind, step // BANKS_PER_CHUNK)]
            columns = slice((step % BANKS_PER_CHUNK) * BANK, (step % BANKS_PER_CHUNK + 1) * BANK)
            nc.tensor.matmul_mx(
                out=bank,
                lhsT=lat_codes[:].bitcast(FP8X4),
                lhsT_scale=lat_scales[:],
                rhs=wu_codes[:, columns].bitcast(FP8X4),
                rhs_scale=wu_scales[:, columns],
                start=True,
                stop=True,
            )

        def store_two_banks(out_view, i, step, result):
            columns = slice((step - 1) * BANK, (step + 1) * BANK)
            nc.sync.dma_start(out=out_view[:, i, columns], in_=result[:, columns])

        def add_products(i, step, products, k_rot):
            heads = slice(step * HEADS_PER_BANK, (step + 1) * HEADS_PER_BANK)
            nc.gpsimd.tensor_tensor(
                out=k_rot[:, heads, :], in0=products[:, :, 0, :], in1=products[:, :, 1, :], op=ALU.add
            )
            if step % 2 == 1:
                store_two_banks(k_out_view, i, step, k_rot[:].rearrange("p h d -> p (h d)"))

        def project_step(i, step, k_rot, v_sb):
            k_bank = psum.tile([P, HEADS_PER_BANK, D], F32, tag="bank")
            project(k_bank[:].rearrange("p h d -> p (h d)"), i, KEYS, step)
            v_bank = psum.tile([P, BANK], F32, tag="bank")
            project(v_bank[:], i, VALUES, step)

            squares = stats.tile([P, HEADS_PER_BANK, D], BF16, tag="squares", bufs=2)
            sumsq = stats.tile([P, HEADS_PER_BANK], F32, tag="sumsq")
            rstd = stats.tile([P, HEADS_PER_BANK], F32, tag="rstd")
            for h in range(HEADS_PER_BANK):
                nc.scalar.activation(
                    out=squares[:, h, :],
                    in_=k_bank[:, h, :],
                    func=ACT.Square,
                    accum_out=sumsq[:, h : h + 1],
                )
            if step != VECTOR_VALUES_STEP:
                nc.scalar.copy(out=v_sb[:, step * BANK : (step + 1) * BANK], in_=v_bank[:])
            nc.scalar.activation(
                out=rstd[:], in_=sumsq[:], func=ACT.Abs_reciprocal_sqrt, scale=1.0 / D, bias=EPS
            )

            products = results.tile([P, HEADS_PER_BANK, 2, D], F32, tag="products", bufs=4)
            for h in range(HEADS_PER_BANK):
                nc.vector.scalar_tensor_tensor(
                    out=products[:, h, :, :].rearrange("p e (j w) -> p (e j) w", w=2),
                    in0=k_bank[:, h, :].unsqueeze(2).to_broadcast([P, D, 2]),
                    scalar=rstd[:, h : h + 1],
                    in1=rope_table[:, i, :, :, :].rearrange("p e j w -> p (e j) w"),
                    op0=ALU.mult,
                    op1=ALU.mult,
                )
            add_products(i, step, products, k_rot)
            if step == VECTOR_VALUES_STEP:
                nc.vector.tensor_copy(out=v_sb[:, step * BANK : (step + 1) * BANK], in_=v_bank[:])
            if step % 2 == 1:
                store_two_banks(v_out_view, i, step, v_sb[:])

        for i in range(TOKEN_TILES):
            k_rot = results.tile([P, HEADS, D], F32, tag="k_rot")
            v_sb = results.tile([P, HEADS * D], F32, tag="v_sb")
            project_step(i, 0, k_rot, v_sb)
            if i + 2 < TOKEN_TILES:
                stage_transpose_x(i + 2)
                stage_quantise_x(i + 2)
            if i + 1 < TOKEN_TILES:
                stage_quantise_latent(i + 1)
            project_step(i, 1, k_rot, v_sb)
            project_step(i, 2, k_rot, v_sb)
            project_step(i, 3, k_rot, v_sb)
            if i + 2 < TOKEN_TILES:
                stage_latent(i + 2)
                stage_round_latent(i + 2)
